import numpy as np
import ml_dtypes


def mxq(x, axis, fmt="e4m3"):
    dtype, down = {"e4m3": (ml_dtypes.float8_e4m3fn, 7), "e5m2": (ml_dtypes.float8_e5m2, 14)}[fmt]
    v = np.moveaxis(np.asarray(x, np.float32).astype(ml_dtypes.bfloat16).astype(np.float64), axis, -1)
    blocks = v.reshape(v.shape[:-1] + (-1, 32))
    amax = np.abs(blocks).max(-1, keepdims=True)
    byte = np.maximum(np.where(amax > 0, np.frexp(amax)[1] - 1 + 127, 0) - down, 1)
    scale = np.exp2(byte - 127.0)
    codes = (blocks / scale).astype(np.float32).astype(dtype).astype(np.float64)
    return np.moveaxis((codes * scale).reshape(v.shape), -1, axis)


WIDE = False


def mx_kscale(k):
    if not WIDE:
        return np.ones(k)
    levels = np.array([18, -18])
    if k % 512:
        return np.exp2(np.random.permutation(np.resize(levels, k // 32))).repeat(32)
    a = np.empty((k // 512, 16))
    for p in range(k // 512):
        a[p, :8] = np.random.permutation(np.resize(levels, 8))
        for g in range(8):
            far = levels[np.abs(levels - a[p, g]) >= 10]
            a[p, g + 8] = far[np.random.randint(len(far))]
    return np.exp2(a.ravel()).repeat(32)


BF16 = ml_dtypes.bfloat16


def bf(x):
    return np.asarray(x, np.float32).astype(BF16)


def f64(x):
    return np.asarray(x).astype(np.float64)


B, S, D, E, WINDOW = 2, 512, 1024, 1024, 10
HALF = WINDOW // 2
T = B * S


def window_softmax(scores):
    i = np.arange(S)[:, None]
    j = np.arange(S)[None, :]
    mask = np.abs(i - j) <= HALF
    scores = np.where(mask[None, :, :], scores, -1e9)
    e = np.exp(scores - scores.max(-1, keepdims=True))
    return e / e.sum(-1, keepdims=True)


def setup_inputs():
    u = mx_kscale(S)
    v = mx_kscale(E)
    s = mx_kscale(T)
    r = np.array([u[max(0, i - HALF):i + HALF + 1].min() for i in range(S)])
    x0 = bf(np.random.standard_normal((B, S, D)))
    Wq0 = bf(np.random.standard_normal((E, D)) / np.sqrt(D))
    bq = bf(np.random.standard_normal(E) * 0.1)
    k0 = bf(np.random.standard_normal((B, S, E)))
    rows = np.exp2(np.random.randint(-6, 1, (B, S, 1))) * 256.0
    g = bf(np.random.standard_normal((B, S, S)) * rows * r[None, :, None] / s.reshape(B, S, 1))
    q0 = f64(x0) @ f64(Wq0).T + f64(bq)
    p = window_softmax(q0 @ f64(k0).transpose(0, 2, 1) / np.sqrt(E))
    return {"x": bf(f64(x0) * s.reshape(B, S, 1)),
            "Wq": bf(f64(Wq0) / v[:, None]),
            "bq": bq,
            "k": bf(f64(k0) * v[None, None, :] / u[None, :, None]),
            "p": np.asarray(p, np.float32),
            "grad_out": g}


def reference(x, Wq, bq, k, p, grad_out):
    pf = f64(p)
    g = f64(grad_out)
    dz2 = pf * (g - (pf * g).sum(-1, keepdims=True))
    dh = mxq(dz2, 2, "e5m2") @ mxq(f64(k), 1, "e4m3")
    dq = (dh / np.sqrt(E)).reshape(T, E)
    dx = (mxq(dq, 1, "e5m2") @ mxq(f64(Wq), 0, "e4m3")).reshape(B, S, D)
    dWq = mxq(dq, 0, "e5m2").T @ mxq(f64(x).reshape(T, D), 0, "e4m3")
    return dx, dWq

from contextlib import ExitStack

import concourse.mybir as mybir
from concourse.masks import make_identity

B, S, D, E = 2, 512, 1024, 1024
HALF = 5
T = B * S
P = 128
WIN = 144
WIN_START = (0, 120, 248, 368)

F32 = mybir.dt.float32
BF16 = mybir.dt.bfloat16
U32 = mybir.dt.uint32
U8 = mybir.dt.uint8
E4M3 = mybir.dt.float8_e4m3fn_x4
E5M2 = mybir.dt.float8_e5m2_x4
MULT = mybir.AluOpType.mult
SUB = mybir.AluOpType.subtract
COPY = mybir.ActivationFunctionType.Copy

FLOPS = 2 * B * S * S * E + 4 * T * E * D
BAND = B * (S * (2 * HALF + 1) - HALF * (HALF + 1))
BYTES = 2 * (T * D + E * D + T * E) + 6 * BAND + 4 * (T * D + E * D)


def tile_localattention_pa_v_kernel(tc, x, Wq, bq, k, p, grad_out, out_0, out_1):
    nc = tc.nc
    with ExitStack() as ctx:
        keep = ctx.enter_context(tc.tile_pool(name="keep", bufs=1))
        outs = ctx.enter_context(tc.tile_pool(name="outs", bufs=16))
        psum = ctx.enter_context(tc.psum_pool(name="psum", bufs=8))
        ctx.enter_context(tc.manual_schedule())

        def tiles(name, shape, dtype, n=2):
            return [keep.tile(shape, dtype, name=f"{name}{i}", tag=f"{name}{i}", align_bytes=64) for i in range(n)]

        ident = keep.tile([P, P], F32, name="ident", tag="ident", align_bytes=64)
        pw = tiles("pw", [P, 4, WIN], F32)
        gw = tiles("gw", [P, 4, WIN], BF16)
        prod = keep.tile([P, 4, WIN], F32, name="prod", tag="prod", align_bytes=64)
        rsum = tiles("rsum", [P, 4], F32)
        dz = tiles("dz", [P, 4, S], BF16)
        dzg = tiles("dzg", [P, S, 4], BF16)
        dzc = tiles("dzc", [P, S], U32)
        dzs = tiles("dzs", [P, S], U8)
        raw, code, scale, grp = {}, {}, {}, {}
        for n in ("k", "w", "x"):
            raw[n] = tiles(n + "raw", [P, 4, 1024], BF16)
        for n in ("k", "w", "x", "b"):
            code[n] = tiles(n + "code", [P, 1024], U32)
            scale[n] = tiles(n + "scale", [P, 1024], U8)
        dqn = tiles("dqn", [P, 4, E], BF16)
        raw["b"] = dqn
        dqc = tiles("dqc", [P, 1024], U32)
        dqs = tiles("dqs", [P, 1024], U8)

        def grouped(n, b):
            if (n, b) not in grp:
                grp[n, b] = keep.tile([P, 4096], BF16, name=f"grp_{n}{b}", tag="grp", bufs=6, align_bytes=64)
            return grp[n, b]

        def bank():
            return psum.tile([P, 512], F32, name="bank", tag="bank")

        def load_window(b):
            for dst, src in ((gw[b], grad_out[b]), (pw[b], p[b])):
                for i in (0, 3):
                    nc.sync.dma_start(out=dst[:, i, :], in_=src[P * i : P * (i + 1), WIN_START[i] : WIN_START[i] + WIN])
                first = P * S + WIN_START[1]
                step = P * S + P
                both = src.rearrange("s j -> (s j)")[first : first + 2 * step].rearrange("(i y) -> i y", i=2)[:, : P * S]
                nc.sync.dma_start(out=dst[:, 1:3, :], in_=both.rearrange("i (r j) -> r i j", j=S)[:, :, :WIN])

        def load(n, b):
            src = {"k": lambda: k[b], "x": lambda: x[b], "w": lambda: Wq[512 * b : 512 * (b + 1), :]}[n]()
            nc.sync.dma_start(out=raw[n][b][:], in_=src.rearrange("(p j) c -> p j c", j=4))

        def softmax_back(b):
            for i in range(4):
                nc.vector.scalar_tensor_tensor(out=prod[:, i, :], in0=gw[b][:, i, :], scalar=1.0, in1=pw[b][:, i, :], op0=MULT, op1=MULT, accum_out=rsum[b][:, i : i + 1])
            for i in range(4):
                cols = slice(WIN_START[i], WIN_START[i] + WIN)
                nc.vector.scalar_tensor_tensor(out=dz[b][:, i, cols], in0=gw[b][:, i, :], scalar=rsum[b][:, i : i + 1], in1=pw[b][:, i, :], op0=SUB, op1=MULT)

        def turn_dz(b):
            banks = []
            for h in range(2):
                t = bank()
                for i in range(2):
                    words = dz[b][:, 2 * h + i, :].bitcast(F32)
                    for u in range(2):
                        at = 256 * u + 128 * i
                        nc.tensor.transpose(t[:, at : at + 128], words[:, u : S // 2 : 2], ident[:])
                banks.append(t)
            return banks

        def take_dz(b, banks, copies):
            words = dzg[b][:].rearrange("p c j -> p (c j)").bitcast(F32).rearrange("p (t m u) -> p t m u", t=4, u=2)
            for h in range(2):
                copies[h](out=words[:, :, 64 * h : 64 * (h + 1), :], in_=banks[h][:].rearrange("p (u m t) -> p t m u", u=2, t=4))

        def quant_dz(b):
            nc.vector.quantize_mx(out=dzc[b][:].bitcast(E5M2), scales=dzs[b][:], in_=dzg[b][:].rearrange("p c j -> p (c j)"))

        def group(n, b, copy, c0, c1):
            copy(
                out=grouped(n, b)[:].rearrange("p (c t) -> p c t", t=4)[:, c0:c1, :].rearrange("p (c i) t -> p c t i", i=4),
                in_=raw[n][b][:, :, c0:c1].rearrange("p t (c i) -> p c t i", i=4),
            )

        def quant(n, b, c0, c1):
            fmt = E5M2 if n == "b" else E4M3
            nc.vector.quantize_mx(
                out=code[n][b][:, c0:c1].bitcast(fmt), scales=scale[n][b][:, c0:c1], in_=grouped(n, b)[:, 4 * c0 : 4 * c1]
            )

        def dh(b, t, h):
            o = bank()
            cols = slice(512 * h, 512 * (h + 1))
            nc.tensor.matmul_mx(
                out=o[:], lhsT=dzc[b][:, P * t : P * (t + 1)].bitcast(E5M2), lhsT_scale=dzs[b][:, P * t : P * (t + 1)],
                rhs=code["k"][b][:, cols].bitcast(E4M3), rhs_scale=scale["k"][b][:, cols], start=True, stop=True)
            return o

        def take_dq(b, t, h, o, eng):
            dst = dqn[b][:, t, 512 * h : 512 * (h + 1)]
            if eng == "A":
                nc.scalar.activation(out=dst, in_=o[:], func=COPY, scale=1.0 / 32.0)
            else:
                nc.vector.tensor_scalar(out=dst, in0=o[:], scalar1=1.0 / 32.0, scalar2=None, op0=MULT)

        def turn_dq(b, t):
            o = bank()
            words = dqn[b][:, t, :].bitcast(F32)
            for g in range(2):
                for u in range(2):
                    at = 256 * g + 128 * u
                    nc.tensor.transpose(o[:, at : at + 128], words[:, 256 * g + u : 256 * (g + 1) : 2], ident[:])
            return o

        def take_turned(b, t, o, copy):
            copy(
                out=grouped("a", b)[:, 1024 * t : 1024 * (t + 1)].bitcast(F32).rearrange("p (g m u) -> p g m u", g=2, u=2),
                in_=o[:].rearrange("p (g u m) -> p g m u", g=2, u=2))

        def quant_dq(b, t0, t1):
            c = slice(256 * t0, 256 * t1)
            nc.vector.quantize_mx(out=dqc[b][:, c].bitcast(E5M2), scales=dqs[b][:, c], in_=grouped("a", b)[:, 1024 * t0 : 1024 * t1])

        def product(lhs, rhs, h):
            o = bank()
            cols = slice(512 * h, 512 * (h + 1))
            for g in range(2):
                lc, ls = lhs[g]
                rc, rs = rhs[g]
                nc.tensor.matmul_mx(out=o[:], lhsT=lc.bitcast(E5M2), lhsT_scale=ls, rhs=rc[:, cols].bitcast(E4M3), rhs_scale=rs[:, cols], start=(g == 0), stop=(g == 1))
            return o

        def out0(b, t, h, copy):
            res = outs.tile([P, 512], F32, name="res", tag="res")
            lhs = [(dqc[b][:, 256 * t + P * g : 256 * t + P * (g + 1)], dqs[b][:, 256 * t + P * g : 256 * t + P * (g + 1)]) for g in range(2)]
            rhs = [(code["w"][g], scale["w"][g]) for g in range(2)]
            o = product(lhs, rhs, h)
            copy(out=res[:], in_=o[:])
            nc.sync.dma_start(out=out_0[b].rearrange("(m t) d -> m t d", t=4)[:, t, 512 * h : 512 * (h + 1)], in_=res[:])

        def out1(e, h, copy):
            res = outs.tile([P, 512], F32, name="res", tag="res")
            cols = slice(P * e, P * (e + 1))
            lhs = [(code["b"][g][:, cols], scale["b"][g][:, cols]) for g in range(2)]
            rhs = [(code["x"][g], scale["x"][g]) for g in range(2)]
            o = product(lhs, rhs, h)
            copy(out=res[:], in_=o[:])
            nc.sync.dma_start(out=out_1[cols, 512 * h : 512 * (h + 1)], in_=res[:])

        V, A = nc.vector.tensor_copy, nc.scalar.copy

        make_identity(nc, ident[:])
        for b in range(2):
            nc.vector.memset(dz[b][:], 0.0)
        load_window(0)
        load("k", 0)
        load_window(1)
        load("k", 1)
        load("w", 0)
        load("w", 1)
        load("x", 0)
        load("x", 1)

        def il(n, b, cs, copy):
            for c in cs:
                group(n, b, copy, 256 * c, 256 * (c + 1))

        def qh(n, b, h):
            quant(n, b, 512 * h, 512 * (h + 1))

        def q(n, b, c0, c1):
            quant(n, b, 256 * c0, 256 * c1)

        softmax_back(0)
        banks = turn_dz(0)
        il("k", 0, (0, 1), V)
        take_dz(0, banks, (A, A))
        il("k", 0, (3, 2), A)
        q("k", 0, 0, 2)
        quant_dz(0)
        softmax_back(1)
        q("k", 0, 2, 4)
        for h in range(2):
            for t in range(4):
                take_dq(0, t, h, dh(0, t, h), "A")
        il("k", 1, (0, 1, 2, 3), V)
        take_dz(1, turn_dz(1), (V, V))
        q("k", 1, 0, 2)
        quant_dz(1)
        q("k", 1, 2, 4)
        for t in range(4):
            take_turned(0, t, turn_dq(0, t), A)
        il("w", 0, (0, 1), V)
        il("w", 1, (0, 1), V)
        q("w", 0, 0, 2)
        quant_dq(0, 0, 2)
        q("w", 1, 0, 2)
        quant_dq(0, 2, 4)
        for h in range(2):
            for t in range(4):
                take_dq(1, t, h, dh(1, t, h), "A")
        for t in range(4):
            out0(0, t, 0, A)
        il("w", 0, (2, 3), V)
        il("w", 1, (2, 3), V)
        for t in range(4):
            take_turned(1, t, turn_dq(1, t), A)
        q("w", 0, 2, 4)
        q("w", 1, 2, 4)
        quant_dq(1, 0, 2)
        quant_dq(1, 2, 4)
        for t in range(4):
            out0(0, t, 1, A)
        il("x", 0, (0, 1, 2, 3), V)
        il("x", 1, (0, 1), V)
        for t in range(4):
            out0(1, t, 0, A)
        q("x", 0, 0, 2)
        il("x", 1, (3,), A)
        q("x", 1, 0, 2)
        il("x", 1, (2,), V)
        il("b", 0, (0,), V)
        q("x", 0, 2, 4)
        il("b", 1, (0,), V)
        for t in range(4):
            out0(1, t, 1, A)
        q("b", 0, 0, 1)
        q("b", 1, 0, 1)
        q("x", 1, 2, 4)
        for c in range(4):
            if c < 3:
                il("b", 0, (c + 1,), V)
                il("b", 1, (c + 1,), V)
                q("b", 0, c + 1, c + 2)
                q("b", 1, c + 1, c + 2)
            for h in range(2):
                for e in (2 * c, 2 * c + 1):
                    out1(e, h, V if c == 3 and e % 2 else A)
